import numpy as np
import ml_dtypes


def mxq(x, axis, fmt="e4m3"):
    dtype, down = {"e4m3": (ml_dtypes.float8_e4m3fn, 7), "e5m2": (ml_dtypes.float8_e5m2, 14)}[fmt]
    v = np.moveaxis(np.asarray(x, np.float32).astype(ml_dtypes.bfloat16).astype(np.float64), axis, -1)
    blocks = v.reshape(v.shape[:-1] + (-1, 32))
    amax = np.abs(blocks).max(-1, keepdims=True)
    byte = np.maximum(np.where(amax > 0, np.frexp(amax)[1] - 1 + 127, 0) - down, 1)
    scale = np.exp2(byte - 127.0)
    codes = (blocks / scale).astype(np.float32).astype(dtype).astype(np.float64)
    return np.moveaxis((codes * scale).reshape(v.shape), -1, axis)


WIDE = False


def mx_kscale(k):
    if not WIDE:
        return np.ones(k)
    levels = np.array([10, -10, 5, -5, 0])
    a = np.random.permutation(np.resize(levels, k // 512 * 4)).reshape(k // 512, 4)
    idx = np.arange(k)
    return np.exp2(a[idx // 512, idx % 128 // 32])


BF16 = ml_dtypes.bfloat16


def bf(x):
    return np.asarray(x, np.float32).astype(BF16)


def f64(x):
    return np.asarray(x).astype(np.float64)


B, DIN, H1, H2, N, I, K, O = 8192, 2048, 1024, 512, 32, 16, 128, 8
KO = K * O
SQ_EPS = 1e-8


def squash(t):
    sq = np.sum(t * t, axis=-1, keepdims=True)
    return (sq / (1.0 + sq)) * t / np.sqrt(sq + SQ_EPS)


def setup_inputs():
    amp = np.exp(0.8 * np.random.standard_normal((B, K, 1)))
    t = np.repeat(np.asarray(mx_kscale(KO))[::O], O)
    h = np.exp2(np.round(np.log2(t) / 2))
    c = h / h.max()
    d = np.where(c < 1.0, 0.0625, 1.0)
    return {"s": bf(np.random.standard_normal((B, K, O)) * amp * 1.4 / np.sqrt(O) * c.reshape(K, O)),
            "Wc": bf(np.random.standard_normal((KO, K)) * 6.0 / np.sqrt(KO) * (d / (c * c))[:, None]),
            "bc": bf(np.random.standard_normal(K) * 0.2)}


def reference(s, Wc, bc):
    v = squash(f64(s)).reshape(B, KO)
    return (mxq(v, 1, "e4m3") @ mxq(f64(Wc), 0, "e4m3")) + f64(bc)

@@ -1,0 +1,154 @@
+from contextlib import ExitStack
+
+import concourse.mybir as mybir
+from concourse.masks import make_identity
+
+F32 = mybir.dt.float32
+BF16 = mybir.dt.bfloat16
+U32 = mybir.dt.uint32
+U8 = mybir.dt.uint8
+FP8X4 = mybir.dt.float8_e4m3fn_x4
+ALU = mybir.AluOpType
+ACT = mybir.ActivationFunctionType
+
+P = 128
+ROWS = 8192
+CAPS = 128
+CAP_LEN = 8
+K = CAPS * CAP_LEN
+N_OUT = 128
+SQ_EPS = 1e-8
+
+SUB = 4
+GROUP_ROWS = P * SUB
+GROUPS = ROWS // GROUP_ROWS
+PASSES = K // (4 * P)
+HALVES = 2
+WORDS = K // 2
+
+FLOPS = 2 * ROWS * K * N_OUT
+
+
+def tile_capsulenetwork_pc_t_kernel(tc, s, Wc, bc, out):
+    nc = tc.nc
+    with ExitStack() as ctx:
+        const = ctx.enter_context(tc.tile_pool(name="const", bufs=1))
+        x_pool = ctx.enter_context(tc.tile_pool(name="x", bufs=4))
+        sq_pool = ctx.enter_context(tc.tile_pool(name="sq", bufs=6))
+        small = ctx.enter_context(tc.tile_pool(name="small", bufs=2))
+        v_pool = ctx.enter_context(tc.tile_pool(name="v", bufs=6))
+        mx_pool = ctx.enter_context(tc.tile_pool(name="mx", bufs=2))
+        res_pool = ctx.enter_context(tc.tile_pool(name="res", bufs=2))
+        q_psum = ctx.enter_context(tc.psum_pool(name="q_psum", bufs=2))
+        f_psum = ctx.enter_context(tc.psum_pool(name="f_psum", bufs=2))
+        t_psum = ctx.enter_context(tc.psum_pool(name="t_psum", bufs=2))
+        o_psum = ctx.enter_context(tc.psum_pool(name="o_psum", bufs=2))
+
+        ident = const.tile([P, P], F32)
+        make_identity(nc, ident[:])
+        one_col = const.tile([P, 1], F32)
+        nc.vector.memset(one_col[:], 1.0)
+
+        bias_bf = const.tile([P, N_OUT], BF16)
+        nc.sync.dma_start(out=bias_bf[:], in_=bc.partition_broadcast(P))
+        bias = const.tile([P, N_OUT], F32)
+        nc.vector.tensor_copy(out=bias[:], in_=bias_bf[:])
+
+        w_raw = const.tile([P, PASSES, 2 * HALVES, N_OUT], BF16)
+        nc.sync.dma_start(
+            out=w_raw[:].rearrange("q c (u e) n -> q (c u) (e n)", u=HALVES),
+            in_=Wc.rearrange("(cu q e) n -> q cu (e n)", q=P, e=2),
+        )
+        w_grouped = const.tile([P, PASSES, N_OUT, 2 * HALVES], BF16, align_bytes=64)
+        nc.vector.tensor_copy(out=w_grouped[:], in_=w_raw[:].rearrange("q c t n -> q c n t"))
+        w_codes = const.tile([P, PASSES, N_OUT], U32, align_bytes=64)
+        w_scales = const.tile([P, PASSES, N_OUT], U8, align_bytes=64)
+        nc.vector.quantize_mx(
+            out=w_codes[:].rearrange("q c n -> q (c n)").bitcast(FP8X4),
+            scales=w_scales[:].rearrange("q c n -> q (c n)"),
+            in_=w_grouped[:].rearrange("q c n t -> q (c n t)"),
+        )
+
+        s_groups = s.rearrange("(g p r) j o -> g p (r j o)", p=P, r=SUB)
+        out_groups = out.rearrange("(g p r) n -> g p (r n)", p=P, r=SUB)
+
+        for g in range(GROUPS):
+            x = x_pool.tile([P, SUB, CAPS, CAP_LEN], BF16)
+            nc.sync.dma_start(out=x[:].rearrange("p r j o -> p (r j o)"), in_=s_groups[g])
+
+            q_t = q_psum.tile([P, SUB, P], F32)
+            for r in range(SUB):
+                sq = sq_pool.tile([P, CAPS, CAP_LEN], F32)
+                nc.scalar.activation(out=sq[:], in_=x[:, r], func=ACT.Square)
+                for o in range(CAP_LEN):
+                    nc.tensor.matmul(
+                        out=q_t[:, r, :],
+                        lhsT=sq[:, :, o],
+                        rhs=ident[:],
+                        is_transpose=True,
+                        start=(o == 0),
+                        stop=(o == CAP_LEN - 1),
+                    )
+
+            one_plus_sq = small.tile([P, SUB, P], F32)
+            nc.scalar.activation(out=one_plus_sq[:], in_=q_t[:], func=ACT.Square, bias=one_col[:, 0:1])
+            denom_sq = small.tile([P, SUB, P], F32)
+            nc.vector.scalar_tensor_tensor(
+                out=denom_sq[:], in0=q_t[:], scalar=SQ_EPS, in1=one_plus_sq[:], op0=ALU.add, op1=ALU.mult
+            )
+            recip = small.tile([P, SUB, P], F32)
+            nc.scalar.activation(out=recip[:], in_=denom_sq[:], func=ACT.Abs_reciprocal_sqrt)
+            f_t = small.tile([P, SUB, P], F32)
+            nc.vector.tensor_tensor(out=f_t[:], in0=q_t[:], in1=recip[:], op=ALU.mult)
+
+            f_rows = f_psum.tile([P, SUB, CAPS], F32)
+            for r in range(SUB):
+                nc.tensor.transpose(out=f_rows[:, r, :], in_=f_t[:, r, :], identity=ident[:])
+
+            grouped = mx_pool.tile([P, SUB, PASSES, P, HALVES], F32, align_bytes=64)
+            for r in range(SUB):
+                v = v_pool.tile([P, CAPS, CAP_LEN], BF16)
+                nc.vector.tensor_tensor(
+                    out=v[:],
+                    in0=x[:, r],
+                    in1=f_rows[:, r, :].unsqueeze(2).to_broadcast([P, CAPS, CAP_LEN]),
+                    op=ALU.mult,
+                )
+                v_words = v[:].rearrange("p j o -> p (j o)").bitcast(F32)
+                v_t = t_psum.tile([P, PASSES, HALVES, P], F32)
+                for c in range(PASSES):
+                    for u in range(HALVES):
+                        first = (c * HALVES + u) * P
+                        nc.tensor.transpose(
+                            out=v_t[:, c, u, :], in_=v_words[:, first : first + P], identity=ident[:]
+                        )
+                nc.scalar.copy(out=grouped[:, r], in_=v_t[:].rearrange("q c u p -> q c p u"))
+
+            codes = mx_pool.tile([P, SUB, PASSES, P], U32, align_bytes=64)
+            scales = mx_pool.tile([P, SUB, PASSES, P], U8, align_bytes=64)
+            nc.vector.quantize_mx(
+                out=codes[:].rearrange("q r c p -> q (r c p)").bitcast(FP8X4),
+                scales=scales[:].rearrange("q r c p -> q (r c p)"),
+                in_=grouped[:].rearrange("q r c p u -> q (r c p u)").bitcast(BF16),
+            )
+
+            acc = o_psum.tile([P, SUB, N_OUT], F32)
+            for r in range(SUB):
+                for c in range(PASSES):
+                    nc.tensor.matmul_mx(
+                        out=acc[:, r, :],
+                        lhsT=codes[:, r, c, :].bitcast(FP8X4),
+                        lhsT_scale=scales[:, r, c, :],
+                        rhs=w_codes[:, c, :].bitcast(FP8X4),
+                        rhs_scale=w_scales[:, c, :],
+                        start=(c == 0),
+                        stop=(c == PASSES - 1),
+                    )
+            res = res_pool.tile([P, SUB, N_OUT], F32)
+            nc.vector.tensor_tensor(
+                out=res[:],
+                in0=acc[:],
+                in1=bias[:].unsqueeze(1).to_broadcast([P, SUB, N_OUT]),
+                op=ALU.add,
+            )
+            nc.sync.dma_start(out=out_groups[g], in_=res[:].rearrange("p r n -> p (r n)"))

@@ -15,16 +15,25 @@ P = 128
 ROWS = 8192
 CAPS = 128
 CAP_LEN = 8
+HALF_CAP = CAP_LEN // 2
 K = CAPS * CAP_LEN
 N_OUT = 128
 SQ_EPS = 1e-8
 
 SUB = 4
-GROUP_ROWS = P * SUB
-GROUPS = ROWS // GROUP_ROWS
+GROUPS = ROWS // (P * SUB)
+TILES = GROUPS * SUB
 PASSES = K // (4 * P)
 HALVES = 2
-WORDS = K // 2
+
+LAG_SUMS = 2
+LAG_FACTOR_A = LAG_SUMS + 1
+LAG_FACTOR_B = LAG_FACTOR_A + 1
+LAG_SCALE = LAG_FACTOR_B + SUB
+LAG_EVACUATE = LAG_SCALE + 1
+LAG_QUANTISE = LAG_EVACUATE + 1
+LAG_FINISH = LAG_QUANTISE + 1
+LOADS_AHEAD = 2
 
 FLOPS = 2 * ROWS * K * N_OUT
 
@@ -33,10 +42,11 @@ def tile_capsulenetwork_pc_t_kernel(tc, s, Wc, bc, out):
     nc = tc.nc
     with ExitStack() as ctx:
         const = ctx.enter_context(tc.tile_pool(name="const", bufs=1))
-        x_pool = ctx.enter_context(tc.tile_pool(name="x", bufs=4))
-        sq_pool = ctx.enter_context(tc.tile_pool(name="sq", bufs=6))
+        x_pool = ctx.enter_context(tc.tile_pool(name="x", bufs=6))
+        sq_pool = ctx.enter_context(tc.tile_pool(name="sq", bufs=3))
+        hs_pool = ctx.enter_context(tc.tile_pool(name="hs", bufs=4))
         small = ctx.enter_context(tc.tile_pool(name="small", bufs=2))
-        v_pool = ctx.enter_context(tc.tile_pool(name="v", bufs=6))
+        v_pool = ctx.enter_context(tc.tile_pool(name="v", bufs=3))
         mx_pool = ctx.enter_context(tc.tile_pool(name="mx", bufs=2))
         res_pool = ctx.enter_context(tc.tile_pool(name="res", bufs=2))
         q_psum = ctx.enter_context(tc.psum_pool(name="q_psum", bufs=2))
@@ -44,94 +54,102 @@ def tile_capsulenetwork_pc_t_kernel(tc, s, Wc, bc, out):
         t_psum = ctx.enter_context(tc.psum_pool(name="t_psum", bufs=2))
         o_psum = ctx.enter_context(tc.psum_pool(name="o_psum", bufs=2))
 
-        ident = const.tile([P, P], F32)
-        make_identity(nc, ident[:])
-        one_col = const.tile([P, 1], F32)
-        nc.vector.memset(one_col[:], 1.0)
-
-        bias_bf = const.tile([P, N_OUT], BF16)
-        nc.sync.dma_start(out=bias_bf[:], in_=bc.partition_broadcast(P))
-        bias = const.tile([P, N_OUT], F32)
-        nc.vector.tensor_copy(out=bias[:], in_=bias_bf[:])
-
-        w_raw = const.tile([P, PASSES, 2 * HALVES, N_OUT], BF16)
-        nc.sync.dma_start(
-            out=w_raw[:].rearrange("q c (u e) n -> q (c u) (e n)", u=HALVES),
-            in_=Wc.rearrange("(cu q e) n -> q cu (e n)", q=P, e=2),
-        )
-        w_grouped = const.tile([P, PASSES, N_OUT, 2 * HALVES], BF16, align_bytes=64)
-        nc.vector.tensor_copy(out=w_grouped[:], in_=w_raw[:].rearrange("q c t n -> q c n t"))
-        w_codes = const.tile([P, PASSES, N_OUT], U32, align_bytes=64)
-        w_scales = const.tile([P, PASSES, N_OUT], U8, align_bytes=64)
-        nc.vector.quantize_mx(
-            out=w_codes[:].rearrange("q c n -> q (c n)").bitcast(FP8X4),
-            scales=w_scales[:].rearrange("q c n -> q (c n)"),
-            in_=w_grouped[:].rearrange("q c n t -> q (c n t)"),
-        )
-
         s_groups = s.rearrange("(g p r) j o -> g p (r j o)", p=P, r=SUB)
         out_groups = out.rearrange("(g p r) n -> g p (r n)", p=P, r=SUB)
 
-        for g in range(GROUPS):
+        x_of = {}
+        hs_of = {}
+        q_of = {}
+        denom_of = {}
+        f_of = {}
+        vt_of = {}
+        grouped_of = {}
+        acc_of = {}
+
+        def load(g):
             x = x_pool.tile([P, SUB, CAPS, CAP_LEN], BF16)
             nc.sync.dma_start(out=x[:].rearrange("p r j o -> p (r j o)"), in_=s_groups[g])
+            x_of[g] = x
 
-            q_t = q_psum.tile([P, SUB, P], F32)
-            for r in range(SUB):
-                sq = sq_pool.tile([P, CAPS, CAP_LEN], F32)
-                nc.scalar.activation(out=sq[:], in_=x[:, r], func=ACT.Square)
-                for o in range(CAP_LEN):
-                    nc.tensor.matmul(
-                        out=q_t[:, r, :],
-                        lhsT=sq[:, :, o],
-                        rhs=ident[:],
-                        is_transpose=True,
-                        start=(o == 0),
-                        stop=(o == CAP_LEN - 1),
-                    )
+        def squares(t):
+            sq = sq_pool.tile([P, CAPS, CAP_LEN], F32)
+            nc.scalar.activation(out=sq[:], in_=x_of[t // SUB][:, t % SUB], func=ACT.Square)
+            hs = hs_pool.tile([P, CAPS, HALF_CAP], F32)
+            nc.gpsimd.tensor_tensor(
+                out=hs[:], in0=sq[:, :, 0:HALF_CAP], in1=sq[:, :, HALF_CAP:CAP_LEN], op=ALU.add
+            )
+            hs_of[t] = hs
 
+        def sums(t):
+            if t % SUB == 0:
+                q_t = q_psum.tile([P, SUB, P], F32)
+                q_of[t // SUB] = q_t
+            hs = hs_of[t]
+            for d in range(HALF_CAP):
+                nc.tensor.matmul(
+                    out=q_of[t // SUB][:, t % SUB, :],
+                    lhsT=hs[:, :, d],
+                    rhs=ident[:],
+                    is_transpose=True,
+                    start=(d == 0),
+                    stop=(d == HALF_CAP - 1),
+                )
+
+        def factor_a(g):
             one_plus_sq = small.tile([P, SUB, P], F32)
-            nc.scalar.activation(out=one_plus_sq[:], in_=q_t[:], func=ACT.Square, bias=one_col[:, 0:1])
+            nc.scalar.activation(
+                out=one_plus_sq[:], in_=q_of[g][:], func=ACT.Square, bias=one_col[:, 0:1]
+            )
             denom_sq = small.tile([P, SUB, P], F32)
             nc.vector.scalar_tensor_tensor(
-                out=denom_sq[:], in0=q_t[:], scalar=SQ_EPS, in1=one_plus_sq[:], op0=ALU.add, op1=ALU.mult
+                out=denom_sq[:], in0=q_of[g][:], scalar=SQ_EPS, in1=one_plus_sq[:], op0=ALU.add, op1=ALU.mult
             )
-            recip = small.tile([P, SUB, P], F32)
-            nc.scalar.activation(out=recip[:], in_=denom_sq[:], func=ACT.Abs_reciprocal_sqrt)
-            f_t = small.tile([P, SUB, P], F32)
-            nc.vector.tensor_tensor(out=f_t[:], in0=q_t[:], in1=recip[:], op=ALU.mult)
+            denom_of[g] = denom_sq
 
+        def factor_b(g):
+            recip = small.tile([P, SUB, P], F32)
+            nc.scalar.activation(out=recip[:], in_=denom_of[g][:], func=ACT.Abs_reciprocal_sqrt)
+            f_t = small.tile([P, SUB, P], F32)
+            nc.vector.tensor_tensor(out=f_t[:], in0=q_of[g][:], in1=recip[:], op=ALU.mult)
             f_rows = f_psum.tile([P, SUB, CAPS], F32)
             for r in range(SUB):
                 nc.tensor.transpose(out=f_rows[:, r, :], in_=f_t[:, r, :], identity=ident[:])
+            f_of[g] = f_rows
 
-            grouped = mx_pool.tile([P, SUB, PASSES, P, HALVES], F32, align_bytes=64)
-            for r in range(SUB):
-                v = v_pool.tile([P, CAPS, CAP_LEN], BF16)
-                nc.vector.tensor_tensor(
-                    out=v[:],
-                    in0=x[:, r],
-                    in1=f_rows[:, r, :].unsqueeze(2).to_broadcast([P, CAPS, CAP_LEN]),
-                    op=ALU.mult,
-                )
-                v_words = v[:].rearrange("p j o -> p (j o)").bitcast(F32)
-                v_t = t_psum.tile([P, PASSES, HALVES, P], F32)
-                for c in range(PASSES):
-                    for u in range(HALVES):
-                        first = (c * HALVES + u) * P
-                        nc.tensor.transpose(
-                            out=v_t[:, c, u, :], in_=v_words[:, first : first + P], identity=ident[:]
-                        )
-                nc.scalar.copy(out=grouped[:, r], in_=v_t[:].rearrange("q c u p -> q c p u"))
+        def scale(t):
+            v = v_pool.tile([P, CAPS, CAP_LEN], BF16)
+            nc.vector.tensor_tensor(
+                out=v[:],
+                in0=x_of[t // SUB][:, t % SUB],
+                in1=f_of[t // SUB][:, t % SUB, :].unsqueeze(2).to_broadcast([P, CAPS, CAP_LEN]),
+                op=ALU.mult,
+            )
+            v_words = v[:].rearrange("p j o -> p (j o)").bitcast(F32)
+            v_t = t_psum.tile([P, PASSES, HALVES, P], F32)
+            for c in range(PASSES):
+                for u in range(HALVES):
+                    first = (c * HALVES + u) * P
+                    nc.tensor.transpose(
+                        out=v_t[:, c, u, :], in_=v_words[:, first : first + P], identity=ident[:]
+                    )
+            vt_of[t] = v_t
 
+        def evacuate(t):
+            if t % SUB == 0:
+                grouped = mx_pool.tile([P, SUB, PASSES, P, HALVES], F32, align_bytes=64)
+                grouped_of[t // SUB] = grouped
+            nc.scalar.copy(
+                out=grouped_of[t // SUB][:, t % SUB], in_=vt_of[t][:].rearrange("q c u p -> q c p u")
+            )
+
+        def quantise(g):
             codes = mx_pool.tile([P, SUB, PASSES, P], U32, align_bytes=64)
             scales = mx_pool.tile([P, SUB, PASSES, P], U8, align_bytes=64)
             nc.vector.quantize_mx(
                 out=codes[:].rearrange("q r c p -> q (r c p)").bitcast(FP8X4),
                 scales=scales[:].rearrange("q r c p -> q (r c p)"),
-                in_=grouped[:].rearrange("q r c p u -> q (r c p u)").bitcast(BF16),
+                in_=grouped_of[g][:].rearrange("q r c p u -> q (r c p u)").bitcast(BF16),
             )
-
             acc = o_psum.tile([P, SUB, N_OUT], F32)
             for r in range(SUB):
                 for c in range(PASSES):
@@ -144,11 +162,63 @@ def tile_capsulenetwork_pc_t_kernel(tc, s, Wc, bc, out):
                         start=(c == 0),
                         stop=(c == PASSES - 1),
                     )
+            acc_of[g] = acc
+
+        def finish(g):
             res = res_pool.tile([P, SUB, N_OUT], F32)
             nc.vector.tensor_tensor(
                 out=res[:],
-                in0=acc[:],
+                in0=acc_of[g][:],
                 in1=bias[:].unsqueeze(1).to_broadcast([P, SUB, N_OUT]),
                 op=ALU.add,
             )
             nc.sync.dma_start(out=out_groups[g], in_=res[:].rearrange("p r n -> p (r n)"))
+
+        for once in range(1):
+            for g in range(LOADS_AHEAD):
+                load(g)
+
+            ident = const.tile([P, P], F32)
+            make_identity(nc, ident[:])
+            one_col = const.tile([P, 1], F32)
+            nc.vector.memset(one_col[:], 1.0)
+
+            bias_bf = const.tile([P, N_OUT], BF16)
+            nc.sync.dma_start(out=bias_bf[:], in_=bc.partition_broadcast(P))
+            bias = const.tile([P, N_OUT], F32)
+            nc.vector.tensor_copy(out=bias[:], in_=bias_bf[:])
+
+            w_raw = const.tile([P, PASSES, 2 * HALVES, N_OUT], BF16)
+            nc.sync.dma_start(
+                out=w_raw[:].rearrange("q c (u e) n -> q (c u) (e n)", u=HALVES),
+                in_=Wc.rearrange("(cu q e) n -> q cu (e n)", q=P, e=2),
+            )
+            w_grouped = const.tile([P, PASSES, N_OUT, 2 * HALVES], BF16, align_bytes=64)
+            nc.vector.tensor_copy(out=w_grouped[:], in_=w_raw[:].rearrange("q c t n -> q c n t"))
+            w_codes = const.tile([P, PASSES, N_OUT], U32, align_bytes=64)
+            w_scales = const.tile([P, PASSES, N_OUT], U8, align_bytes=64)
+            nc.vector.quantize_mx(
+                out=w_codes[:].rearrange("q c n -> q (c n)").bitcast(FP8X4),
+                scales=w_scales[:].rearrange("q c n -> q (c n)"),
+                in_=w_grouped[:].rearrange("q c n t -> q (c n t)"),
+            )
+
+            for step in range(TILES + LAG_FINISH):
+                if 0 <= step - LAG_SUMS < TILES:
+                    sums(step - LAG_SUMS)
+                if 0 <= step - LAG_SCALE < TILES:
+                    scale(step - LAG_SCALE)
+                if 0 <= step - LAG_EVACUATE < TILES:
+                    evacuate(step - LAG_EVACUATE)
+                if 0 <= step - LAG_QUANTISE < TILES and (step - LAG_QUANTISE) % SUB == SUB - 1:
+                    quantise((step - LAG_QUANTISE) // SUB)
+                if 0 <= step - LAG_FINISH < TILES and (step - LAG_FINISH) % SUB == SUB - 1:
+                    finish((step - LAG_FINISH) // SUB)
+                if 0 <= step - LAG_FACTOR_B < TILES and (step - LAG_FACTOR_B) % SUB == SUB - 1:
+                    factor_b((step - LAG_FACTOR_B) // SUB)
+                if 0 <= step - LAG_FACTOR_A < TILES and (step - LAG_FACTOR_A) % SUB == SUB - 1:
+                    factor_a((step - LAG_FACTOR_A) // SUB)
+                if step < TILES:
+                    squares(step)
+                    if step % SUB == 0 and step // SUB + LOADS_AHEAD < GROUPS:
+                        load(step // SUB + LOADS_AHEAD)

@@ -26,14 +26,18 @@ TILES = GROUPS * SUB
 PASSES = K // (4 * P)
 HALVES = 2
 
-LAG_SUMS = 2
-LAG_FACTOR_A = LAG_SUMS + 1
-LAG_FACTOR_B = LAG_FACTOR_A + 1
-LAG_SCALE = LAG_FACTOR_B + SUB
-LAG_EVACUATE = LAG_SCALE + 1
+LOADS_AHEAD = 8
+LAG_SUMS = 3
+LAG_ONE_PLUS = LAG_SUMS + 1
+LAG_DENOM = LAG_ONE_PLUS + 1
+LAG_RECIP = LAG_DENOM + 1
+LAG_FACTOR = LAG_RECIP + 1
+LAG_SCALE = LAG_FACTOR + SUB
+LAG_TRANSPOSE = LAG_SCALE + 1
+LAG_EVACUATE = LAG_TRANSPOSE + 1
 LAG_QUANTISE = LAG_EVACUATE + 1
-LAG_FINISH = LAG_QUANTISE + 1
-LOADS_AHEAD = 2
+LAG_MULTIPLY = LAG_QUANTISE + 1
+LAG_FINISH = LAG_MULTIPLY + 1
 
 FLOPS = 2 * ROWS * K * N_OUT
 
@@ -42,38 +46,43 @@ def tile_capsulenetwork_pc_t_kernel(tc, s, Wc, bc, out):
     nc = tc.nc
     with ExitStack() as ctx:
         const = ctx.enter_context(tc.tile_pool(name="const", bufs=1))
-        x_pool = ctx.enter_context(tc.tile_pool(name="x", bufs=6))
+        x_pool = ctx.enter_context(tc.tile_pool(name="x", bufs=LOADS_AHEAD + LAG_SCALE + 3))
         sq_pool = ctx.enter_context(tc.tile_pool(name="sq", bufs=3))
-        hs_pool = ctx.enter_context(tc.tile_pool(name="hs", bufs=4))
+        hs_pool = ctx.enter_context(tc.tile_pool(name="hs", bufs=LAG_SUMS + 2))
         small = ctx.enter_context(tc.tile_pool(name="small", bufs=2))
-        v_pool = ctx.enter_context(tc.tile_pool(name="v", bufs=3))
+        v_pool = ctx.enter_context(tc.tile_pool(name="v", bufs=4))
         mx_pool = ctx.enter_context(tc.tile_pool(name="mx", bufs=2))
         res_pool = ctx.enter_context(tc.tile_pool(name="res", bufs=2))
-        q_psum = ctx.enter_context(tc.psum_pool(name="q_psum", bufs=2))
+        q_psum = ctx.enter_context(tc.psum_pool(name="q_psum", bufs=3))
         f_psum = ctx.enter_context(tc.psum_pool(name="f_psum", bufs=2))
         t_psum = ctx.enter_context(tc.psum_pool(name="t_psum", bufs=2))
-        o_psum = ctx.enter_context(tc.psum_pool(name="o_psum", bufs=2))
+        o_psum = ctx.enter_context(tc.psum_pool(name="o_psum", bufs=1))
 
-        s_groups = s.rearrange("(g p r) j o -> g p (r j o)", p=P, r=SUB)
+        s_tiles = s.rearrange("(g p r) j o -> g r p (j o)", p=P, r=SUB)
         out_groups = out.rearrange("(g p r) n -> g p (r n)", p=P, r=SUB)
 
         x_of = {}
         hs_of = {}
         q_of = {}
+        one_plus_of = {}
         denom_of = {}
+        recip_of = {}
         f_of = {}
+        v_of = {}
         vt_of = {}
         grouped_of = {}
+        codes_of = {}
+        scales_of = {}
         acc_of = {}
 
-        def load(g):
-            x = x_pool.tile([P, SUB, CAPS, CAP_LEN], BF16)
-            nc.sync.dma_start(out=x[:].rearrange("p r j o -> p (r j o)"), in_=s_groups[g])
-            x_of[g] = x
+        def load(t):
+            x = x_pool.tile([P, CAPS, CAP_LEN], BF16)
+            nc.sync.dma_start(out=x[:].rearrange("p j o -> p (j o)"), in_=s_tiles[t // SUB, t % SUB])
+            x_of[t] = x
 
         def squares(t):
             sq = sq_pool.tile([P, CAPS, CAP_LEN], F32)
-            nc.scalar.activation(out=sq[:], in_=x_of[t // SUB][:, t % SUB], func=ACT.Square)
+            nc.scalar.activation(out=sq[:], in_=x_of[t][:], func=ACT.Square)
             hs = hs_pool.tile([P, CAPS, HALF_CAP], F32)
             nc.gpsimd.tensor_tensor(
                 out=hs[:], in0=sq[:, :, 0:HALF_CAP], in1=sq[:, :, HALF_CAP:CAP_LEN], op=ALU.add
@@ -84,33 +93,36 @@ def tile_capsulenetwork_pc_t_kernel(tc, s, Wc, bc, out):
             if t % SUB == 0:
                 q_t = q_psum.tile([P, SUB, P], F32)
                 q_of[t // SUB] = q_t
-            hs = hs_of[t]
             for d in range(HALF_CAP):
                 nc.tensor.matmul(
                     out=q_of[t // SUB][:, t % SUB, :],
-                    lhsT=hs[:, :, d],
+                    lhsT=hs_of[t][:, :, d],
                     rhs=ident[:],
                     is_transpose=True,
                     start=(d == 0),
                     stop=(d == HALF_CAP - 1),
                 )
 
-        def factor_a(g):
+        def one_plus(g):
             one_plus_sq = small.tile([P, SUB, P], F32)
-            nc.scalar.activation(
-                out=one_plus_sq[:], in_=q_of[g][:], func=ACT.Square, bias=one_col[:, 0:1]
-            )
+            nc.scalar.activation(out=one_plus_sq[:], in_=q_of[g][:], func=ACT.Square, bias=one_col[:, 0:1])
+            one_plus_of[g] = one_plus_sq
+
+        def denom(g):
             denom_sq = small.tile([P, SUB, P], F32)
             nc.vector.scalar_tensor_tensor(
-                out=denom_sq[:], in0=q_of[g][:], scalar=SQ_EPS, in1=one_plus_sq[:], op0=ALU.add, op1=ALU.mult
+                out=denom_sq[:], in0=q_of[g][:], scalar=SQ_EPS, in1=one_plus_of[g][:], op0=ALU.add, op1=ALU.mult
             )
             denom_of[g] = denom_sq
 
-        def factor_b(g):
-            recip = small.tile([P, SUB, P], F32)
-            nc.scalar.activation(out=recip[:], in_=denom_of[g][:], func=ACT.Abs_reciprocal_sqrt)
+        def recip(g):
+            recip_t = small.tile([P, SUB, P], F32)
+            nc.scalar.activation(out=recip_t[:], in_=denom_of[g][:], func=ACT.Abs_reciprocal_sqrt)
+            recip_of[g] = recip_t
+
+        def factor(g):
             f_t = small.tile([P, SUB, P], F32)
-            nc.vector.tensor_tensor(out=f_t[:], in0=q_of[g][:], in1=recip[:], op=ALU.mult)
+            nc.vector.tensor_tensor(out=f_t[:], in0=q_of[g][:], in1=recip_of[g][:], op=ALU.mult)
             f_rows = f_psum.tile([P, SUB, CAPS], F32)
             for r in range(SUB):
                 nc.tensor.transpose(out=f_rows[:, r, :], in_=f_t[:, r, :], identity=ident[:])
@@ -120,11 +132,14 @@ def tile_capsulenetwork_pc_t_kernel(tc, s, Wc, bc, out):
             v = v_pool.tile([P, CAPS, CAP_LEN], BF16)
             nc.vector.tensor_tensor(
                 out=v[:],
-                in0=x_of[t // SUB][:, t % SUB],
+                in0=x_of[t][:],
                 in1=f_of[t // SUB][:, t % SUB, :].unsqueeze(2).to_broadcast([P, CAPS, CAP_LEN]),
                 op=ALU.mult,
             )
-            v_words = v[:].rearrange("p j o -> p (j o)").bitcast(F32)
+            v_of[t] = v
+
+        def transpose(t):
+            v_words = v_of[t][:].rearrange("p j o -> p (j o)").bitcast(F32)
             v_t = t_psum.tile([P, PASSES, HALVES, P], F32)
             for c in range(PASSES):
                 for u in range(HALVES):
@@ -150,13 +165,17 @@ def tile_capsulenetwork_pc_t_kernel(tc, s, Wc, bc, out):
                 scales=scales[:].rearrange("q r c p -> q (r c p)"),
                 in_=grouped_of[g][:].rearrange("q r c p u -> q (r c p u)").bitcast(BF16),
             )
+            codes_of[g] = codes
+            scales_of[g] = scales
+
+        def multiply(g):
             acc = o_psum.tile([P, SUB, N_OUT], F32)
             for r in range(SUB):
                 for c in range(PASSES):
                     nc.tensor.matmul_mx(
                         out=acc[:, r, :],
-                        lhsT=codes[:, r, c, :].bitcast(FP8X4),
-                        lhsT_scale=scales[:, r, c, :],
+                        lhsT=codes_of[g][:, r, c, :].bitcast(FP8X4),
+                        lhsT_scale=scales_of[g][:, r, c, :],
                         rhs=w_codes[:, c, :].bitcast(FP8X4),
                         rhs_scale=w_scales[:, c, :],
                         start=(c == 0),
@@ -174,9 +193,17 @@ def tile_capsulenetwork_pc_t_kernel(tc, s, Wc, bc, out):
             )
             nc.sync.dma_start(out=out_groups[g], in_=res[:].rearrange("p r n -> p (r n)"))
 
-        for once in range(1):
-            for g in range(LOADS_AHEAD):
-                load(g)
+        def for_tile(stage, t):
+            if 0 <= t < TILES:
+                stage(t)
+
+        def for_group(stage, t):
+            if 0 <= t < TILES and t % SUB == SUB - 1:
+                stage(t // SUB)
+
+        with tc.manual_schedule():
+            for t in range(LOADS_AHEAD):
+                load(t)
 
             ident = const.tile([P, P], F32)
             make_identity(nc, ident[:])
@@ -204,21 +231,16 @@ def tile_capsulenetwork_pc_t_kernel(tc, s, Wc, bc, out):
             )
 
             for step in range(TILES + LAG_FINISH):
-                if 0 <= step - LAG_SUMS < TILES:
-                    sums(step - LAG_SUMS)
-                if 0 <= step - LAG_SCALE < TILES:
-                    scale(step - LAG_SCALE)
-                if 0 <= step - LAG_EVACUATE < TILES:
-                    evacuate(step - LAG_EVACUATE)
-                if 0 <= step - LAG_QUANTISE < TILES and (step - LAG_QUANTISE) % SUB == SUB - 1:
-                    quantise((step - LAG_QUANTISE) // SUB)
-                if 0 <= step - LAG_FINISH < TILES and (step - LAG_FINISH) % SUB == SUB - 1:
-                    finish((step - LAG_FINISH) // SUB)
-                if 0 <= step - LAG_FACTOR_B < TILES and (step - LAG_FACTOR_B) % SUB == SUB - 1:
-                    factor_b((step - LAG_FACTOR_B) // SUB)
-                if 0 <= step - LAG_FACTOR_A < TILES and (step - LAG_FACTOR_A) % SUB == SUB - 1:
-                    factor_a((step - LAG_FACTOR_A) // SUB)
-                if step < TILES:
-                    squares(step)
-                    if step % SUB == 0 and step // SUB + LOADS_AHEAD < GROUPS:
-                        load(step // SUB + LOADS_AHEAD)
+                for_tile(sums, step - LAG_SUMS)
+                for_group(factor, step - LAG_FACTOR)
+                for_group(denom, step - LAG_DENOM)
+                for_tile(scale, step - LAG_SCALE)
+                for_tile(transpose, step - LAG_TRANSPOSE)
+                for_tile(evacuate, step - LAG_EVACUATE)
+                for_group(quantise, step - LAG_QUANTISE)
+                for_group(multiply, step - LAG_MULTIPLY)
+                for_group(finish, step - LAG_FINISH)
+                for_group(recip, step - LAG_RECIP)
+                for_group(one_plus, step - LAG_ONE_PLUS)
+                for_tile(squares, step)
+                for_tile(load, step + LOADS_AHEAD)

@@ -20,7 +20,7 @@ K = CAPS * CAP_LEN
 N_OUT = 128
 SQ_EPS = 1e-8
 
-SUB = 4
+SUB = 2
 GROUPS = ROWS // (P * SUB)
 TILES = GROUPS * SUB
 PASSES = K // (4 * P)

@@ -25,6 +25,7 @@ GROUPS = ROWS // (P * SUB)
 TILES = GROUPS * SUB
 PASSES = K // (4 * P)
 HALVES = 2
+GPSIMD_EVERY = 4
 
 LOADS_AHEAD = 8
 LAG_SUMS = 3
@@ -49,6 +50,7 @@ def tile_capsulenetwork_pc_t_kernel(tc, s, Wc, bc, out):
         x_pool = ctx.enter_context(tc.tile_pool(name="x", bufs=LOADS_AHEAD + LAG_SCALE + 3))
         sq_pool = ctx.enter_context(tc.tile_pool(name="sq", bufs=3))
         hs_pool = ctx.enter_context(tc.tile_pool(name="hs", bufs=LAG_SUMS + 2))
+        sq8_pool = ctx.enter_context(tc.tile_pool(name="sq8", bufs=2))
         small = ctx.enter_context(tc.tile_pool(name="small", bufs=2))
         v_pool = ctx.enter_context(tc.tile_pool(name="v", bufs=4))
         mx_pool = ctx.enter_context(tc.tile_pool(name="mx", bufs=2))
@@ -81,26 +83,32 @@ def tile_capsulenetwork_pc_t_kernel(tc, s, Wc, bc, out):
             x_of[t] = x
 
         def squares(t):
-            sq = sq_pool.tile([P, CAPS, CAP_LEN], F32)
-            nc.scalar.activation(out=sq[:], in_=x_of[t][:], func=ACT.Square)
-            hs = hs_pool.tile([P, CAPS, HALF_CAP], F32)
-            nc.gpsimd.tensor_tensor(
-                out=hs[:], in0=sq[:, :, 0:HALF_CAP], in1=sq[:, :, HALF_CAP:CAP_LEN], op=ALU.add
-            )
-            hs_of[t] = hs
+            if t % GPSIMD_EVERY == GPSIMD_EVERY - 1:
+                sq8 = sq8_pool.tile([P, CAPS, CAP_LEN], F32)
+                nc.gpsimd.tensor_tensor(out=sq8[:], in0=x_of[t][:], in1=x_of[t][:], op=ALU.mult)
+                hs_of[t] = sq8
+            else:
+                sq = sq_pool.tile([P, CAPS, CAP_LEN], F32)
+                nc.scalar.activation(out=sq[:], in_=x_of[t][:], func=ACT.Square)
+                hs = hs_pool.tile([P, CAPS, HALF_CAP], F32)
+                nc.gpsimd.tensor_tensor(
+                    out=hs[:], in0=sq[:, :, 0:HALF_CAP], in1=sq[:, :, HALF_CAP:CAP_LEN], op=ALU.add
+                )
+                hs_of[t] = hs
 
         def sums(t):
             if t % SUB == 0:
                 q_t = q_psum.tile([P, SUB, P], F32)
                 q_of[t // SUB] = q_t
-            for d in range(HALF_CAP):
+            planes = hs_of[t].shape[2]
+            for d in range(planes):
                 nc.tensor.matmul(
                     out=q_of[t // SUB][:, t % SUB, :],
                     lhsT=hs_of[t][:, :, d],
                     rhs=ident[:],
                     is_transpose=True,
                     start=(d == 0),
-                    stop=(d == HALF_CAP - 1),
+                    stop=(d == planes - 1),
                 )
 
         def one_plus(g):

from contextlib import ExitStack

import concourse.mybir as mybir
from concourse.masks import make_identity

F32 = mybir.dt.float32
BF16 = mybir.dt.bfloat16
U32 = mybir.dt.uint32
U8 = mybir.dt.uint8
FP8X4 = mybir.dt.float8_e4m3fn_x4
ALU = mybir.AluOpType
ACT = mybir.ActivationFunctionType

P = 128
ROWS = 8192
CAPS = 128
CAP_LEN = 8
HALF_CAP = CAP_LEN // 2
K = CAPS * CAP_LEN
N_OUT = 128
SQ_EPS = 1e-8

SUB = 2
GROUPS = ROWS // (P * SUB)
TILES = GROUPS * SUB
PASSES = K // (4 * P)
HALVES = 2
GPSIMD_EVERY = 4

LOADS_AHEAD = 8
LAG_SUMS = 3
LAG_ONE_PLUS = LAG_SUMS + 1
LAG_DENOM = LAG_ONE_PLUS + 1
LAG_RECIP = LAG_DENOM + 1
LAG_FACTOR = LAG_RECIP + 1
LAG_SCALE = LAG_FACTOR + SUB
LAG_TRANSPOSE = LAG_SCALE + 1
LAG_EVACUATE = LAG_TRANSPOSE + 1
LAG_QUANTISE = LAG_EVACUATE + 1
LAG_MULTIPLY = LAG_QUANTISE + 1
LAG_FINISH = LAG_MULTIPLY + 1

FLOPS = 2 * ROWS * K * N_OUT


def tile_capsulenetwork_pc_t_kernel(tc, s, Wc, bc, out):
    nc = tc.nc
    with ExitStack() as ctx:
        const = ctx.enter_context(tc.tile_pool(name="const", bufs=1))
        x_pool = ctx.enter_context(tc.tile_pool(name="x", bufs=LOADS_AHEAD + LAG_SCALE + 3))
        sq_pool = ctx.enter_context(tc.tile_pool(name="sq", bufs=3))
        hs_pool = ctx.enter_context(tc.tile_pool(name="hs", bufs=LAG_SUMS + 2))
        sq8_pool = ctx.enter_context(tc.tile_pool(name="sq8", bufs=2))
        small = ctx.enter_context(tc.tile_pool(name="small", bufs=2))
        v_pool = ctx.enter_context(tc.tile_pool(name="v", bufs=4))
        mx_pool = ctx.enter_context(tc.tile_pool(name="mx", bufs=2))
        res_pool = ctx.enter_context(tc.tile_pool(name="res", bufs=2))
        q_psum = ctx.enter_context(tc.psum_pool(name="q_psum", bufs=3))
        f_psum = ctx.enter_context(tc.psum_pool(name="f_psum", bufs=2))
        t_psum = ctx.enter_context(tc.psum_pool(name="t_psum", bufs=2))
        o_psum = ctx.enter_context(tc.psum_pool(name="o_psum", bufs=1))

        s_tiles = s.rearrange("(g p r) j o -> g r p (j o)", p=P, r=SUB)
        out_groups = out.rearrange("(g p r) n -> g p (r n)", p=P, r=SUB)

        x_of = {}
        hs_of = {}
        q_of = {}
        one_plus_of = {}
        denom_of = {}
        recip_of = {}
        f_of = {}
        v_of = {}
        vt_of = {}
        grouped_of = {}
        codes_of = {}
        scales_of = {}
        acc_of = {}

        def load(t):
            x = x_pool.tile([P, CAPS, CAP_LEN], BF16)
            nc.sync.dma_start(out=x[:].rearrange("p j o -> p (j o)"), in_=s_tiles[t // SUB, t % SUB])
            x_of[t] = x

        def squares(t):
            if t % GPSIMD_EVERY == GPSIMD_EVERY - 1:
                sq8 = sq8_pool.tile([P, CAPS, CAP_LEN], F32)
                nc.gpsimd.tensor_tensor(out=sq8[:], in0=x_of[t][:], in1=x_of[t][:], op=ALU.mult)
                hs_of[t] = sq8
            else:
                sq = sq_pool.tile([P, CAPS, CAP_LEN], F32)
                nc.scalar.activation(out=sq[:], in_=x_of[t][:], func=ACT.Square)
                hs = hs_pool.tile([P, CAPS, HALF_CAP], F32)
                nc.gpsimd.tensor_tensor(
                    out=hs[:], in0=sq[:, :, 0:HALF_CAP], in1=sq[:, :, HALF_CAP:CAP_LEN], op=ALU.add
                )
                hs_of[t] = hs

        def sums(t):
            if t % SUB == 0:
                q_t = q_psum.tile([P, SUB, P], F32)
                q_of[t // SUB] = q_t
            planes = hs_of[t].shape[2]
            for d in range(planes):
                nc.tensor.matmul(
                    out=q_of[t // SUB][:, t % SUB, :],
                    lhsT=hs_of[t][:, :, d],
                    rhs=ident[:],
                    is_transpose=True,
                    start=(d == 0),
                    stop=(d == planes - 1),
                )

        def one_plus(g):
            one_plus_sq = small.tile([P, SUB, P], F32)
            nc.scalar.activation(out=one_plus_sq[:], in_=q_of[g][:], func=ACT.Square, bias=one_col[:, 0:1])
            one_plus_of[g] = one_plus_sq

        def denom(g):
            denom_sq = small.tile([P, SUB, P], F32)
            nc.vector.scalar_tensor_tensor(
                out=denom_sq[:], in0=q_of[g][:], scalar=SQ_EPS, in1=one_plus_of[g][:], op0=ALU.add, op1=ALU.mult
            )
            denom_of[g] = denom_sq

        def recip(g):
            recip_t = small.tile([P, SUB, P], F32)
            nc.scalar.activation(out=recip_t[:], in_=denom_of[g][:], func=ACT.Abs_reciprocal_sqrt)
            recip_of[g] = recip_t

        def factor(g):
            f_t = small.tile([P, SUB, P], F32)
            nc.vector.tensor_tensor(out=f_t[:], in0=q_of[g][:], in1=recip_of[g][:], op=ALU.mult)
            f_rows = f_psum.tile([P, SUB, CAPS], F32)
            for r in range(SUB):
                nc.tensor.transpose(out=f_rows[:, r, :], in_=f_t[:, r, :], identity=ident[:])
            f_of[g] = f_rows

        def scale(t):
            v = v_pool.tile([P, CAPS, CAP_LEN], BF16)
            nc.vector.tensor_tensor(
                out=v[:],
                in0=x_of[t][:],
                in1=f_of[t // SUB][:, t % SUB, :].unsqueeze(2).to_broadcast([P, CAPS, CAP_LEN]),
                op=ALU.mult,
            )
            v_of[t] = v

        def transpose(t):
            v_words = v_of[t][:].rearrange("p j o -> p (j o)").bitcast(F32)
            v_t = t_psum.tile([P, PASSES, HALVES, P], F32)
            for c in range(PASSES):
                for u in range(HALVES):
                    first = (c * HALVES + u) * P
                    nc.tensor.transpose(
                        out=v_t[:, c, u, :], in_=v_words[:, first : first + P], identity=ident[:]
                    )
            vt_of[t] = v_t

        def evacuate(t):
            if t % SUB == 0:
                grouped = mx_pool.tile([P, SUB, PASSES, P, HALVES], F32, align_bytes=64)
                grouped_of[t // SUB] = grouped
            nc.scalar.copy(
                out=grouped_of[t // SUB][:, t % SUB], in_=vt_of[t][:].rearrange("q c u p -> q c p u")
            )

        def quantise(g):
            codes = mx_pool.tile([P, SUB, PASSES, P], U32, align_bytes=64)
            scales = mx_pool.tile([P, SUB, PASSES, P], U8, align_bytes=64)
            nc.vector.quantize_mx(
                out=codes[:].rearrange("q r c p -> q (r c p)").bitcast(FP8X4),
                scales=scales[:].rearrange("q r c p -> q (r c p)"),
                in_=grouped_of[g][:].rearrange("q r c p u -> q (r c p u)").bitcast(BF16),
            )
            codes_of[g] = codes
            scales_of[g] = scales

        def multiply(g):
            acc = o_psum.tile([P, SUB, N_OUT], F32)
            for r in range(SUB):
                for c in range(PASSES):
                    nc.tensor.matmul_mx(
                        out=acc[:, r, :],
                        lhsT=codes_of[g][:, r, c, :].bitcast(FP8X4),
                        lhsT_scale=scales_of[g][:, r, c, :],
                        rhs=w_codes[:, c, :].bitcast(FP8X4),
                        rhs_scale=w_scales[:, c, :],
                        start=(c == 0),
                        stop=(c == PASSES - 1),
                    )
            acc_of[g] = acc

        def finish(g):
            res = res_pool.tile([P, SUB, N_OUT], F32)
            nc.vector.tensor_tensor(
                out=res[:],
                in0=acc_of[g][:],
                in1=bias[:].unsqueeze(1).to_broadcast([P, SUB, N_OUT]),
                op=ALU.add,
            )
            nc.sync.dma_start(out=out_groups[g], in_=res[:].rearrange("p r n -> p (r n)"))

        def for_tile(stage, t):
            if 0 <= t < TILES:
                stage(t)

        def for_group(stage, t):
            if 0 <= t < TILES and t % SUB == SUB - 1:
                stage(t // SUB)

        with tc.manual_schedule():
            for t in range(LOADS_AHEAD):
                load(t)

            ident = const.tile([P, P], F32)
            make_identity(nc, ident[:])
            one_col = const.tile([P, 1], F32)
            nc.vector.memset(one_col[:], 1.0)

            bias_bf = const.tile([P, N_OUT], BF16)
            nc.sync.dma_start(out=bias_bf[:], in_=bc.partition_broadcast(P))
            bias = const.tile([P, N_OUT], F32)
            nc.vector.tensor_copy(out=bias[:], in_=bias_bf[:])

            w_raw = const.tile([P, PASSES, 2 * HALVES, N_OUT], BF16)
            nc.sync.dma_start(
                out=w_raw[:].rearrange("q c (u e) n -> q (c u) (e n)", u=HALVES),
                in_=Wc.rearrange("(cu q e) n -> q cu (e n)", q=P, e=2),
            )
            w_grouped = const.tile([P, PASSES, N_OUT, 2 * HALVES], BF16, align_bytes=64)
            nc.vector.tensor_copy(out=w_grouped[:], in_=w_raw[:].rearrange("q c t n -> q c n t"))
            w_codes = const.tile([P, PASSES, N_OUT], U32, align_bytes=64)
            w_scales = const.tile([P, PASSES, N_OUT], U8, align_bytes=64)
            nc.vector.quantize_mx(
                out=w_codes[:].rearrange("q c n -> q (c n)").bitcast(FP8X4),
                scales=w_scales[:].rearrange("q c n -> q (c n)"),
                in_=w_grouped[:].rearrange("q c n t -> q (c n t)"),
            )

            for step in range(TILES + LAG_FINISH):
                for_tile(sums, step - LAG_SUMS)
                for_group(factor, step - LAG_FACTOR)
                for_group(denom, step - LAG_DENOM)
                for_tile(scale, step - LAG_SCALE)
                for_tile(transpose, step - LAG_TRANSPOSE)
                for_tile(evacuate, step - LAG_EVACUATE)
                for_group(quantise, step - LAG_QUANTISE)
                for_group(multiply, step - LAG_MULTIPLY)
                for_group(finish, step - LAG_FINISH)
                for_group(recip, step - LAG_RECIP)
                for_group(one_plus, step - LAG_ONE_PLUS)
                for_tile(squares, step)
                for_tile(load, step + LOADS_AHEAD)
